import numpy as np
import ml_dtypes

BF16 = ml_dtypes.bfloat16


def bf(x):
    return np.asarray(x, np.float32).astype(BF16)


def f32(x):
    return np.asarray(x, np.float32)


def f64(x):
    return np.asarray(x).astype(np.float64)


def striped(idx):
    return np.tile(idx.reshape(-1, 16).T, (8, 1))


D, S, M, N, T, H = 128, 4096, 128, 1024, 2, 512


def setup_inputs():
    return {
        "table": bf(np.random.standard_normal((D, S))),
        "w0": bf(np.random.standard_normal((D, M)) / np.sqrt(T * D)),
        "w1": bf(np.random.standard_normal((D, M)) / np.sqrt(T * D)),
        "cb": f32(0.1 * np.random.standard_normal((M, 1))),
        "wk": bf(np.random.standard_normal((M, M)) / np.sqrt(M)),
        "bk": f32(0.1 * np.random.standard_normal((M, 1))),
        "wv": bf(np.random.standard_normal((M, M)) / np.sqrt(M)),
        "bv": f32(0.1 * np.random.standard_normal((M, 1))),
        "offs": striped(np.random.permutation(np.tile(np.arange(S), 2))[:N]),
    }


def reference(table, w0, w1, cb, wk, bk, wv, bv, offs):
    idx = offs[:16].T.reshape(-1)
    t = f64(table)
    fi = f64(w0).T @ t[:, idx[:H]] + f64(w1).T @ t[:, idx[H:]] + f64(cb)
    return np.concatenate([f64(wk).T @ fi + f64(bk), f64(wv).T @ fi + f64(bv)], axis=0)

@@ -1,0 +1,58 @@
+import concourse.mybir as mybir
+
+BF16, F32, U16 = mybir.dt.bfloat16, mybir.dt.float32, mybir.dt.uint16
+ADD = mybir.AluOpType.add
+IDENTITY = mybir.ActivationFunctionType.Identity
+
+P = 128
+WORDS = 4096
+PAIRS = 512
+TAPS = 2
+PER_COLUMN = 16
+
+FLOPS = 2 * P * P * PAIRS * TAPS + 2 * P * (2 * P) * PAIRS
+
+
+def tile_ehemb_kernel(tc, table, w0, w1, cb, wk, bk, wv, bv, offs, out):
+    nc = tc.nc
+    with (
+        tc.tile_pool(name="held", bufs=1) as held,
+        tc.psum_pool(name="banks", bufs=1) as banks,
+    ):
+        offsets = held.tile([P, TAPS * PAIRS // PER_COLUMN], U16, name="offsets")
+        nc.sync.dma_start(offsets[:], offs)
+        words = held.tile([P, WORDS], BF16, name="words")
+        nc.sync.dma_start(words[:], table)
+
+        tap0 = held.tile([P, P], BF16, name="tap0")
+        tap1 = held.tile([P, P], BF16, name="tap1")
+        to_keys = held.tile([P, P], BF16, name="to_keys")
+        to_values = held.tile([P, P], BF16, name="to_values")
+        for tile, source in ((tap0, w0), (tap1, w1), (to_keys, wk), (to_values, wv)):
+            nc.scalar.dma_start(tile[:], source)
+
+        conv_bias = held.tile([P, 1], F32, name="conv_bias")
+        key_bias = held.tile([P, 1], F32, name="key_bias")
+        value_bias = held.tile([P, 1], F32, name="value_bias")
+        for tile, source in ((conv_bias, cb), (key_bias, bk), (value_bias, bv)):
+            nc.gpsimd.dma_start(tile[:], source)
+
+        columns = PAIRS // PER_COLUMN
+        conv = banks.tile([P, PAIRS], F32, name="conv")
+        nc.tensor.matmul(conv[:], tap0[:], words[:].indirect(offsets[:, 0:columns]), start=True, stop=False)
+        nc.tensor.matmul(conv[:], tap1[:], words[:].indirect(offsets[:, columns : 2 * columns]), start=False, stop=True)
+
+        fi = held.tile([P, PAIRS], BF16, name="fi")
+        nc.vector.tensor_scalar(fi[:], conv[:], conv_bias[:], None, ADD)
+
+        keys_bank = banks.tile([P, PAIRS], F32, name="keys_bank")
+        values_bank = banks.tile([P, PAIRS], F32, name="values_bank")
+        nc.tensor.matmul(keys_bank[:], to_keys[:], fi[:], start=True, stop=True)
+        nc.tensor.matmul(values_bank[:], to_values[:], fi[:], start=True, stop=True)
+
+        keys = held.tile([P, PAIRS], F32, name="keys")
+        values = held.tile([P, PAIRS], F32, name="values")
+        nc.vector.tensor_scalar(keys[:], keys_bank[:], key_bias[:], None, ADD)
+        nc.scalar.activation(values[:], values_bank[:], IDENTITY, bias=value_bias[:])
+        nc.sync.dma_start(out[0:P, :], keys[:])
+        nc.scalar.dma_start(out[P : 2 * P, :], values[:])

@@ -20,22 +20,21 @@ def tile_ehemb_kernel(tc, table, w0, w1, cb, wk, bk, wv, bv, offs, out):
         tc.psum_pool(name="banks", bufs=1) as banks,
     ):
         offsets = held.tile([P, TAPS * PAIRS // PER_COLUMN], U16, name="offsets")
-        nc.sync.dma_start(offsets[:], offs)
         words = held.tile([P, WORDS], BF16, name="words")
-        nc.sync.dma_start(words[:], table)
-
         tap0 = held.tile([P, P], BF16, name="tap0")
         tap1 = held.tile([P, P], BF16, name="tap1")
         to_keys = held.tile([P, P], BF16, name="to_keys")
         to_values = held.tile([P, P], BF16, name="to_values")
-        for tile, source in ((tap0, w0), (tap1, w1), (to_keys, wk), (to_values, wv)):
-            nc.scalar.dma_start(tile[:], source)
-
         conv_bias = held.tile([P, 1], F32, name="conv_bias")
         key_bias = held.tile([P, 1], F32, name="key_bias")
         value_bias = held.tile([P, 1], F32, name="value_bias")
-        for tile, source in ((conv_bias, cb), (key_bias, bk), (value_bias, bv)):
-            nc.gpsimd.dma_start(tile[:], source)
+
+        nc.scalar.dma_start(words[:], table)
+        for tile, source in ((to_keys, wk), (to_values, wv), (key_bias, bk), (value_bias, bv)):
+            nc.scalar.dma_start(tile[:], source)
+        nc.sync.dma_start(offsets[:], offs)
+        for tile, source in ((tap0, w0), (tap1, w1), (conv_bias, cb)):
+            nc.sync.dma_start(tile[:], source)
 
         columns = PAIRS // PER_COLUMN
         conv = banks.tile([P, PAIRS], F32, name="conv")

@@ -9,6 +9,8 @@ WORDS = 4096
 PAIRS = 512
 TAPS = 2
 PER_COLUMN = 16
+HALF = PAIRS // 2
+WARM_UPS = 10
 
 FLOPS = 2 * P * P * PAIRS * TAPS + 2 * P * (2 * P) * PAIRS
 
@@ -17,7 +19,9 @@ def tile_ehemb_kernel(tc, table, w0, w1, cb, wk, bk, wv, bv, offs, out):
     nc = tc.nc
     with (
         tc.tile_pool(name="held", bufs=1) as held,
+        tc.tile_pool(name="steps", bufs=2) as steps,
         tc.psum_pool(name="banks", bufs=1) as banks,
+        tc.psum_pool(name="step_banks", bufs=2) as step_banks,
     ):
         offsets = held.tile([P, TAPS * PAIRS // PER_COLUMN], U16, name="offsets")
         words = held.tile([P, WORDS], BF16, name="words")
@@ -36,22 +40,36 @@ def tile_ehemb_kernel(tc, table, w0, w1, cb, wk, bk, wv, bv, offs, out):
         for tile, source in ((tap0, w0), (tap1, w1), (conv_bias, cb)):
             nc.sync.dma_start(tile[:], source)
 
+
+        scratch = held.tile([P, 1], F32, name="scratch")
+        nc.vector.memset(scratch[:], 0.0)
+        nc.scalar.activation(scratch[:], scratch[:], IDENTITY)
+
+        zeros = held.tile([P, PAIRS], BF16, name="zeros")
+        nc.vector.memset(zeros[:], 0.0)
+        unread = banks.tile([P, PAIRS], F32, name="unread")
+        for i in range(WARM_UPS):
+            nc.tensor.matmul(unread[:], zeros[:, 0:P], zeros[:], start=True, stop=True)
+
         columns = PAIRS // PER_COLUMN
         conv = banks.tile([P, PAIRS], F32, name="conv")
         nc.tensor.matmul(conv[:], tap0[:], words[:].indirect(offsets[:, 0:columns]), start=True, stop=False)
         nc.tensor.matmul(conv[:], tap1[:], words[:].indirect(offsets[:, columns : 2 * columns]), start=False, stop=True)
 
-        fi = held.tile([P, PAIRS], BF16, name="fi")
-        nc.vector.tensor_scalar(fi[:], conv[:], conv_bias[:], None, ADD)
+        for h in range(PAIRS // HALF):
+            positions = slice(h * HALF, (h + 1) * HALF)
 
-        keys_bank = banks.tile([P, PAIRS], F32, name="keys_bank")
-        values_bank = banks.tile([P, PAIRS], F32, name="values_bank")
-        nc.tensor.matmul(keys_bank[:], to_keys[:], fi[:], start=True, stop=True)
-        nc.tensor.matmul(values_bank[:], to_values[:], fi[:], start=True, stop=True)
+            fi = steps.tile([P, HALF], BF16, name="fi")
+            nc.vector.tensor_scalar(fi[:], conv[:, positions], conv_bias[:], None, ADD)
 
-        keys = held.tile([P, PAIRS], F32, name="keys")
-        values = held.tile([P, PAIRS], F32, name="values")
-        nc.vector.tensor_scalar(keys[:], keys_bank[:], key_bias[:], None, ADD)
-        nc.scalar.activation(values[:], values_bank[:], IDENTITY, bias=value_bias[:])
-        nc.sync.dma_start(out[0:P, :], keys[:])
-        nc.scalar.dma_start(out[P : 2 * P, :], values[:])
+            keys_bank = step_banks.tile([P, HALF], F32, name="keys_bank")
+            values_bank = step_banks.tile([P, HALF], F32, name="values_bank")
+            nc.tensor.matmul(keys_bank[:], to_keys[:], fi[:], start=True, stop=True)
+            nc.tensor.matmul(values_bank[:], to_values[:], fi[:], start=True, stop=True)
+
+            keys = steps.tile([P, HALF], F32, name="keys")
+            values = steps.tile([P, HALF], F32, name="values")
+            nc.scalar.activation(keys[:], keys_bank[:], IDENTITY, bias=key_bias[:])
+            nc.vector.tensor_scalar(values[:], values_bank[:], value_bias[:], None, ADD)
+            nc.sync.dma_start(out[0:P, positions], keys[:])
+            nc.sync.dma_start(out[P : 2 * P, positions], values[:])

@@ -10,7 +10,6 @@ PAIRS = 512
 TAPS = 2
 PER_COLUMN = 16
 HALF = PAIRS // 2
-WARM_UPS = 10
 
 FLOPS = 2 * P * P * PAIRS * TAPS + 2 * P * (2 * P) * PAIRS
 
@@ -44,12 +43,6 @@ def tile_ehemb_kernel(tc, table, w0, w1, cb, wk, bk, wv, bv, offs, out):
         scratch = held.tile([P, 1], F32, name="scratch")
         nc.vector.memset(scratch[:], 0.0)
         nc.scalar.activation(scratch[:], scratch[:], IDENTITY)
-
-        zeros = held.tile([P, PAIRS], BF16, name="zeros")
-        nc.vector.memset(zeros[:], 0.0)
-        unread = banks.tile([P, PAIRS], F32, name="unread")
-        for i in range(WARM_UPS):
-            nc.tensor.matmul(unread[:], zeros[:, 0:P], zeros[:], start=True, stop=True)
 
         columns = PAIRS // PER_COLUMN
         conv = banks.tile([P, PAIRS], F32, name="conv")

@@ -19,7 +19,7 @@ def tile_ehemb_kernel(tc, table, w0, w1, cb, wk, bk, wv, bv, offs, out):
     with (
         tc.tile_pool(name="held", bufs=1) as held,
         tc.tile_pool(name="steps", bufs=2) as steps,
-        tc.psum_pool(name="banks", bufs=1) as banks,
+        tc.psum_pool(name="tap_banks", bufs=2) as tap_banks,
         tc.psum_pool(name="step_banks", bufs=2) as step_banks,
     ):
         offsets = held.tile([P, TAPS * PAIRS // PER_COLUMN], U16, name="offsets")
@@ -44,21 +44,31 @@ def tile_ehemb_kernel(tc, table, w0, w1, cb, wk, bk, wv, bv, offs, out):
         nc.vector.memset(scratch[:], 0.0)
         nc.scalar.activation(scratch[:], scratch[:], IDENTITY)
 
-        columns = PAIRS // PER_COLUMN
-        conv = banks.tile([P, PAIRS], F32, name="conv")
-        nc.tensor.matmul(conv[:], tap0[:], words[:].indirect(offsets[:, 0:columns]), start=True, stop=False)
-        nc.tensor.matmul(conv[:], tap1[:], words[:].indirect(offsets[:, columns : 2 * columns]), start=False, stop=True)
+        columns = HALF // PER_COLUMN
+        pieces = range(PAIRS // HALF)
+        first_taps = [tap_banks.tile([P, HALF], F32, name="first_tap") for h in pieces]
+        second_taps = [tap_banks.tile([P, HALF], F32, name="second_tap") for h in pieces]
+        for t, (tap, products) in enumerate(((tap0, first_taps), (tap1, second_taps))):
+            for h in pieces:
+                piece = (t * len(pieces) + h) * columns
+                picked = words[:].indirect(offsets[:, piece : piece + columns])
+                nc.tensor.matmul(products[h][:], tap[:], picked, start=True, stop=True)
 
-        for h in range(PAIRS // HALF):
+        biased = [steps.tile([P, HALF], F32, name="biased") for h in pieces]
+        for h in pieces:
+            nc.scalar.activation(biased[h][:], first_taps[h][:], IDENTITY, bias=conv_bias[:])
+
+        fis = [steps.tile([P, HALF], BF16, name="fi") for h in pieces]
+        for h in pieces:
+            nc.vector.tensor_tensor(fis[h][:], second_taps[h][:], biased[h][:], ADD)
+
+        for h in pieces:
             positions = slice(h * HALF, (h + 1) * HALF)
-
-            fi = steps.tile([P, HALF], BF16, name="fi")
-            nc.vector.tensor_scalar(fi[:], conv[:, positions], conv_bias[:], None, ADD)
 
             keys_bank = step_banks.tile([P, HALF], F32, name="keys_bank")
             values_bank = step_banks.tile([P, HALF], F32, name="values_bank")
-            nc.tensor.matmul(keys_bank[:], to_keys[:], fi[:], start=True, stop=True)
-            nc.tensor.matmul(values_bank[:], to_values[:], fi[:], start=True, stop=True)
+            nc.tensor.matmul(keys_bank[:], to_keys[:], fis[h][:], start=True, stop=True)
+            nc.tensor.matmul(values_bank[:], to_values[:], fis[h][:], start=True, stop=True)
 
             keys = steps.tile([P, HALF], F32, name="keys")
             values = steps.tile([P, HALF], F32, name="values")

@@ -33,12 +33,17 @@ def tile_ehemb_kernel(tc, table, w0, w1, cb, wk, bk, wv, bv, offs, out):
         value_bias = held.tile([P, 1], F32, name="value_bias")
 
         nc.scalar.dma_start(words[:], table)
-        for tile, source in ((to_keys, wk), (to_values, wv), (key_bias, bk), (value_bias, bv)):
-            nc.scalar.dma_start(tile[:], source)
         nc.sync.dma_start(offsets[:], offs)
-        for tile, source in ((tap0, w0), (tap1, w1), (conv_bias, cb)):
+        for tile, source in (
+            (tap0, w0),
+            (conv_bias, cb),
+            (tap1, w1),
+            (to_keys, wk),
+            (to_values, wv),
+            (key_bias, bk),
+            (value_bias, bv),
+        ):
             nc.sync.dma_start(tile[:], source)
-
 
         scratch = held.tile([P, 1], F32, name="scratch")
         nc.vector.memset(scratch[:], 0.0)

@@ -9,7 +9,10 @@ WORDS = 4096
 PAIRS = 512
 TAPS = 2
 PER_COLUMN = 16
-HALF = PAIRS // 2
+PIECE = 128
+PIECES = PAIRS // PIECE
+STORED = 2
+BANKS = 8
 
 FLOPS = 2 * P * P * PAIRS * TAPS + 2 * P * (2 * P) * PAIRS
 
@@ -18,9 +21,9 @@ def tile_ehemb_kernel(tc, table, w0, w1, cb, wk, bk, wv, bv, offs, out):
     nc = tc.nc
     with (
         tc.tile_pool(name="held", bufs=1) as held,
-        tc.tile_pool(name="steps", bufs=2) as steps,
-        tc.psum_pool(name="tap_banks", bufs=2) as tap_banks,
-        tc.psum_pool(name="step_banks", bufs=2) as step_banks,
+        tc.tile_pool(name="steps", bufs=PIECES) as steps,
+        tc.tile_pool(name="staged", bufs=PIECES // STORED) as staged,
+        tc.psum_pool(name="banks", bufs=BANKS) as banks,
     ):
         offsets = held.tile([P, TAPS * PAIRS // PER_COLUMN], U16, name="offsets")
         words = held.tile([P, WORDS], BF16, name="words")
@@ -49,35 +52,36 @@ def tile_ehemb_kernel(tc, table, w0, w1, cb, wk, bk, wv, bv, offs, out):
         nc.vector.memset(scratch[:], 0.0)
         nc.scalar.activation(scratch[:], scratch[:], IDENTITY)
 
-        columns = HALF // PER_COLUMN
-        pieces = range(PAIRS // HALF)
-        first_taps = [tap_banks.tile([P, HALF], F32, name="first_tap") for h in pieces]
-        second_taps = [tap_banks.tile([P, HALF], F32, name="second_tap") for h in pieces]
+        columns = PIECE // PER_COLUMN
+        pieces = range(PIECES)
+        first_taps = [banks.tile([P, PIECE], F32, name="first_tap", tag="bank") for i in pieces]
+        second_taps = [banks.tile([P, PIECE], F32, name="second_tap", tag="bank") for i in pieces]
         for t, (tap, products) in enumerate(((tap0, first_taps), (tap1, second_taps))):
-            for h in pieces:
-                piece = (t * len(pieces) + h) * columns
+            for i in pieces:
+                piece = (t * PIECES + i) * columns
                 picked = words[:].indirect(offsets[:, piece : piece + columns])
-                nc.tensor.matmul(products[h][:], tap[:], picked, start=True, stop=True)
+                nc.tensor.matmul(products[i][:], tap[:], picked, start=True, stop=True)
 
-        biased = [steps.tile([P, HALF], F32, name="biased") for h in pieces]
-        for h in pieces:
-            nc.scalar.activation(biased[h][:], first_taps[h][:], IDENTITY, bias=conv_bias[:])
+        biased = [steps.tile([P, PIECE], F32, name="biased") for i in pieces]
+        for i in pieces:
+            nc.scalar.activation(biased[i][:], first_taps[i][:], IDENTITY, bias=conv_bias[:])
 
-        fis = [steps.tile([P, HALF], BF16, name="fi") for h in pieces]
-        for h in pieces:
-            nc.vector.tensor_tensor(fis[h][:], second_taps[h][:], biased[h][:], ADD)
+        fis = [steps.tile([P, PIECE], BF16, name="fi") for i in pieces]
+        for i in pieces:
+            nc.vector.tensor_tensor(fis[i][:], second_taps[i][:], biased[i][:], ADD)
 
-        for h in pieces:
-            positions = slice(h * HALF, (h + 1) * HALF)
-
-            keys_bank = step_banks.tile([P, HALF], F32, name="keys_bank")
-            values_bank = step_banks.tile([P, HALF], F32, name="values_bank")
-            nc.tensor.matmul(keys_bank[:], to_keys[:], fis[h][:], start=True, stop=True)
-            nc.tensor.matmul(values_bank[:], to_values[:], fis[h][:], start=True, stop=True)
-
-            keys = steps.tile([P, HALF], F32, name="keys")
-            values = steps.tile([P, HALF], F32, name="values")
-            nc.scalar.activation(keys[:], keys_bank[:], IDENTITY, bias=key_bias[:])
-            nc.vector.tensor_scalar(values[:], values_bank[:], value_bias[:], None, ADD)
+        for group in range(PIECES // STORED):
+            keys = staged.tile([P, STORED * PIECE], F32, name="keys")
+            values = staged.tile([P, STORED * PIECE], F32, name="values")
+            for s in range(STORED):
+                fi = fis[group * STORED + s]
+                part = slice(s * PIECE, (s + 1) * PIECE)
+                keys_bank = banks.tile([P, PIECE], F32, name="keys_bank", tag="bank")
+                values_bank = banks.tile([P, PIECE], F32, name="values_bank", tag="bank")
+                nc.tensor.matmul(keys_bank[:], to_keys[:], fi[:], start=True, stop=True)
+                nc.tensor.matmul(values_bank[:], to_values[:], fi[:], start=True, stop=True)
+                nc.scalar.activation(keys[:, part], keys_bank[:], IDENTITY, bias=key_bias[:])
+                nc.vector.tensor_scalar(values[:, part], values_bank[:], value_bias[:], None, ADD)
+            positions = slice(group * STORED * PIECE, (group + 1) * STORED * PIECE)
             nc.sync.dma_start(out[0:P, positions], keys[:])
             nc.sync.dma_start(out[P : 2 * P, positions], values[:])

@@ -9,6 +9,7 @@ WORDS = 4096
 PAIRS = 512
 TAPS = 2
 PER_COLUMN = 16
+WIDE = 256
 PIECE = 128
 PIECES = PAIRS // PIECE
 STORED = 2
@@ -52,23 +53,22 @@ def tile_ehemb_kernel(tc, table, w0, w1, cb, wk, bk, wv, bv, offs, out):
         nc.vector.memset(scratch[:], 0.0)
         nc.scalar.activation(scratch[:], scratch[:], IDENTITY)
 
-        columns = PIECE // PER_COLUMN
-        pieces = range(PIECES)
-        first_taps = [banks.tile([P, PIECE], F32, name="first_tap", tag="bank") for i in pieces]
-        second_taps = [banks.tile([P, PIECE], F32, name="second_tap", tag="bank") for i in pieces]
-        for t, (tap, products) in enumerate(((tap0, first_taps), (tap1, second_taps))):
-            for i in pieces:
-                piece = (t * PIECES + i) * columns
-                picked = words[:].indirect(offsets[:, piece : piece + columns])
-                nc.tensor.matmul(products[i][:], tap[:], picked, start=True, stop=True)
+        first_taps = [banks.tile([P, WIDE], F32, name="first_tap", tag="bank") for w in range(PAIRS // WIDE)]
+        second_taps = [banks.tile([P, PIECE], F32, name="second_tap", tag="bank") for i in range(PIECES)]
+        for tap, entry, products in ((tap0, 0, first_taps), (tap1, PAIRS, second_taps)):
+            for product in products:
+                entries = product.shape[1]
+                picked = words[:].indirect(offsets[:, entry // PER_COLUMN : (entry + entries) // PER_COLUMN])
+                nc.tensor.matmul(product[:], tap[:], picked, start=True, stop=True)
+                entry += entries
 
-        biased = [steps.tile([P, PIECE], F32, name="biased") for i in pieces]
-        for i in pieces:
-            nc.scalar.activation(biased[i][:], first_taps[i][:], IDENTITY, bias=conv_bias[:])
+        biased = held.tile([P, PAIRS], F32, name="biased")
+        for w, product in enumerate(first_taps):
+            nc.scalar.activation(biased[:, w * WIDE : (w + 1) * WIDE], product[:], IDENTITY, bias=conv_bias[:])
 
-        fis = [steps.tile([P, PIECE], BF16, name="fi") for i in pieces]
-        for i in pieces:
-            nc.vector.tensor_tensor(fis[i][:], second_taps[i][:], biased[i][:], ADD)
+        fis = [steps.tile([P, PIECE], BF16, name="fi") for i in range(PIECES)]
+        for i, product in enumerate(second_taps):
+            nc.vector.tensor_tensor(fis[i][:], product[:], biased[:, i * PIECE : (i + 1) * PIECE], ADD)
 
         for group in range(PIECES // STORED):
             keys = staged.tile([P, STORED * PIECE], F32, name="keys")

@@ -14,6 +14,7 @@ PIECE = 128
 PIECES = PAIRS // PIECE
 STORED = 2
 BANKS = 8
+WARM_UPS = 6
 
 FLOPS = 2 * P * P * PAIRS * TAPS + 2 * P * (2 * P) * PAIRS
 
@@ -52,6 +53,12 @@ def tile_ehemb_kernel(tc, table, w0, w1, cb, wk, bk, wv, bv, offs, out):
         scratch = held.tile([P, 1], F32, name="scratch")
         nc.vector.memset(scratch[:], 0.0)
         nc.scalar.activation(scratch[:], scratch[:], IDENTITY)
+
+        zeros = held.tile([P, PAIRS], BF16, name="zeros")
+        nc.vector.memset(zeros[:], 0.0)
+        unread = banks.tile([P, PAIRS], F32, name="unread", tag="bank")
+        for i in range(WARM_UPS):
+            nc.tensor.matmul(unread[:], zeros[:, 0:P], zeros[:], start=True, stop=True)
 
         first_taps = [banks.tile([P, WIDE], F32, name="first_tap", tag="bank") for w in range(PAIRS // WIDE)]
         second_taps = [banks.tile([P, PIECE], F32, name="second_tap", tag="bank") for i in range(PIECES)]

@@ -9,7 +9,6 @@ WORDS = 4096
 PAIRS = 512
 TAPS = 2
 PER_COLUMN = 16
-WIDE = 256
 PIECE = 128
 PIECES = PAIRS // PIECE
 STORED = 2
@@ -60,22 +59,23 @@ def tile_ehemb_kernel(tc, table, w0, w1, cb, wk, bk, wv, bv, offs, out):
         for i in range(WARM_UPS):
             nc.tensor.matmul(unread[:], zeros[:, 0:P], zeros[:], start=True, stop=True)
 
-        first_taps = [banks.tile([P, WIDE], F32, name="first_tap", tag="bank") for w in range(PAIRS // WIDE)]
-        second_taps = [banks.tile([P, PIECE], F32, name="second_tap", tag="bank") for i in range(PIECES)]
-        for tap, entry, products in ((tap0, 0, first_taps), (tap1, PAIRS, second_taps)):
-            for product in products:
-                entries = product.shape[1]
-                picked = words[:].indirect(offsets[:, entry // PER_COLUMN : (entry + entries) // PER_COLUMN])
-                nc.tensor.matmul(product[:], tap[:], picked, start=True, stop=True)
-                entry += entries
+        columns = PIECE // PER_COLUMN
+        pieces = range(PIECES)
+        taps = (tap0, tap1)
+        products = {}
+        for t, i in [(t, 0) for t in range(TAPS)] + [(t, i) for t in range(TAPS) for i in pieces[1:]]:
+            products[t, i] = banks.tile([P, PIECE], F32, name="product", tag="bank")
+            piece = (t * PIECES + i) * columns
+            picked = words[:].indirect(offsets[:, piece : piece + columns])
+            nc.tensor.matmul(products[t, i][:], taps[t][:], picked, start=True, stop=True)
 
-        biased = held.tile([P, PAIRS], F32, name="biased")
-        for w, product in enumerate(first_taps):
-            nc.scalar.activation(biased[:, w * WIDE : (w + 1) * WIDE], product[:], IDENTITY, bias=conv_bias[:])
+        biased = [steps.tile([P, PIECE], F32, name="biased") for i in pieces]
+        for i in pieces:
+            nc.scalar.activation(biased[i][:], products[0, i][:], IDENTITY, bias=conv_bias[:])
 
-        fis = [steps.tile([P, PIECE], BF16, name="fi") for i in range(PIECES)]
-        for i, product in enumerate(second_taps):
-            nc.vector.tensor_tensor(fis[i][:], product[:], biased[:, i * PIECE : (i + 1) * PIECE], ADD)
+        fis = [steps.tile([P, PIECE], BF16, name="fi") for i in pieces]
+        for i in pieces:
+            nc.vector.tensor_tensor(fis[i][:], products[1, i][:], biased[i][:], ADD)
 
         for group in range(PIECES // STORED):
             keys = staged.tile([P, STORED * PIECE], F32, name="keys")

@@ -63,7 +63,10 @@ def tile_ehemb_kernel(tc, table, w0, w1, cb, wk, bk, wv, bv, offs, out):
         pieces = range(PIECES)
         taps = (tap0, tap1)
         products = {}
-        for t, i in [(t, 0) for t in range(TAPS)] + [(t, i) for t in range(TAPS) for i in pieces[1:]]:
+        first_taps = [(0, i) for i in pieces]
+        second_taps = [(1, i) for i in pieces]
+        in_turn = [look_up for pair in zip(first_taps[1:], second_taps[:-1]) for look_up in pair]
+        for t, i in first_taps[:1] + in_turn + second_taps[-1:]:
             products[t, i] = banks.tile([P, PIECE], F32, name="product", tag="bank")
             piece = (t * PIECES + i) * columns
             picked = words[:].indirect(offsets[:, piece : piece + columns])

@@ -63,10 +63,8 @@ def tile_ehemb_kernel(tc, table, w0, w1, cb, wk, bk, wv, bv, offs, out):
         pieces = range(PIECES)
         taps = (tap0, tap1)
         products = {}
-        first_taps = [(0, i) for i in pieces]
-        second_taps = [(1, i) for i in pieces]
-        in_turn = [look_up for pair in zip(first_taps[1:], second_taps[:-1]) for look_up in pair]
-        for t, i in first_taps[:1] + in_turn + second_taps[-1:]:
+        by_pairs = [(t, i) for first in pieces[::2] for t in range(TAPS) for i in (first, first + 1)]
+        for t, i in by_pairs:
             products[t, i] = banks.tile([P, PIECE], F32, name="product", tag="bank")
             piece = (t * PIECES + i) * columns
             picked = words[:].indirect(offsets[:, piece : piece + columns])

@@ -91,5 +91,6 @@ def tile_ehemb_kernel(tc, table, w0, w1, cb, wk, bk, wv, bv, offs, out):
                 nc.scalar.activation(keys[:, part], keys_bank[:], IDENTITY, bias=key_bias[:])
                 nc.vector.tensor_scalar(values[:, part], values_bank[:], value_bias[:], None, ADD)
             positions = slice(group * STORED * PIECE, (group + 1) * STORED * PIECE)
-            nc.sync.dma_start(out[0:P, positions], keys[:])
+            keys_queue = nc.scalar if group == PIECES // STORED - 1 else nc.sync
+            keys_queue.dma_start(out[0:P, positions], keys[:])
             nc.sync.dma_start(out[P : 2 * P, positions], values[:])

@@ -36,10 +36,12 @@ def tile_ehemb_kernel(tc, table, w0, w1, cb, wk, bk, wv, bv, offs, out):
         key_bias = held.tile([P, 1], F32, name="key_bias")
         value_bias = held.tile([P, 1], F32, name="value_bias")
 
-        nc.scalar.dma_start(words[:], table)
+        half = WORDS // 2
+        nc.scalar.dma_start(words[:, :half], table[:, :half])
         nc.sync.dma_start(offsets[:], offs)
+        nc.sync.dma_start(tap0[:], w0)
+        nc.sync.dma_start(words[:, half:], table[:, half:])
         for tile, source in (
-            (tap0, w0),
             (conv_bias, cb),
             (tap1, w1),
             (to_keys, wk),

import concourse.mybir as mybir

BF16, F32, U16 = mybir.dt.bfloat16, mybir.dt.float32, mybir.dt.uint16
ADD = mybir.AluOpType.add
IDENTITY = mybir.ActivationFunctionType.Identity

P = 128
WORDS = 4096
PAIRS = 512
TAPS = 2
PER_COLUMN = 16
PIECE = 128
PIECES = PAIRS // PIECE
STORED = 2
BANKS = 8
WARM_UPS = 6

FLOPS = 2 * P * P * PAIRS * TAPS + 2 * P * (2 * P) * PAIRS


def tile_ehemb_kernel(tc, table, w0, w1, cb, wk, bk, wv, bv, offs, out):
    nc = tc.nc
    with (
        tc.tile_pool(name="held", bufs=1) as held,
        tc.tile_pool(name="steps", bufs=PIECES) as steps,
        tc.tile_pool(name="staged", bufs=PIECES // STORED) as staged,
        tc.psum_pool(name="banks", bufs=BANKS) as banks,
    ):
        offsets = held.tile([P, TAPS * PAIRS // PER_COLUMN], U16, name="offsets")
        words = held.tile([P, WORDS], BF16, name="words")
        tap0 = held.tile([P, P], BF16, name="tap0")
        tap1 = held.tile([P, P], BF16, name="tap1")
        to_keys = held.tile([P, P], BF16, name="to_keys")
        to_values = held.tile([P, P], BF16, name="to_values")
        conv_bias = held.tile([P, 1], F32, name="conv_bias")
        key_bias = held.tile([P, 1], F32, name="key_bias")
        value_bias = held.tile([P, 1], F32, name="value_bias")

        half = WORDS // 2
        nc.scalar.dma_start(words[:, :half], table[:, :half])
        nc.sync.dma_start(offsets[:], offs)
        nc.sync.dma_start(tap0[:], w0)
        nc.sync.dma_start(words[:, half:], table[:, half:])
        for tile, source in (
            (conv_bias, cb),
            (tap1, w1),
            (to_keys, wk),
            (to_values, wv),
            (key_bias, bk),
            (value_bias, bv),
        ):
            nc.sync.dma_start(tile[:], source)

        scratch = held.tile([P, 1], F32, name="scratch")
        nc.vector.memset(scratch[:], 0.0)
        nc.scalar.activation(scratch[:], scratch[:], IDENTITY)

        zeros = held.tile([P, PAIRS], BF16, name="zeros")
        nc.vector.memset(zeros[:], 0.0)
        unread = banks.tile([P, PAIRS], F32, name="unread", tag="bank")
        for i in range(WARM_UPS):
            nc.tensor.matmul(unread[:], zeros[:, 0:P], zeros[:], start=True, stop=True)

        columns = PIECE // PER_COLUMN
        pieces = range(PIECES)
        taps = (tap0, tap1)
        products = {}
        by_pairs = [(t, i) for first in pieces[::2] for t in range(TAPS) for i in (first, first + 1)]
        for t, i in by_pairs:
            products[t, i] = banks.tile([P, PIECE], F32, name="product", tag="bank")
            piece = (t * PIECES + i) * columns
            picked = words[:].indirect(offsets[:, piece : piece + columns])
            nc.tensor.matmul(products[t, i][:], taps[t][:], picked, start=True, stop=True)

        biased = [steps.tile([P, PIECE], F32, name="biased") for i in pieces]
        for i in pieces:
            nc.scalar.activation(biased[i][:], products[0, i][:], IDENTITY, bias=conv_bias[:])

        fis = [steps.tile([P, PIECE], BF16, name="fi") for i in pieces]
        for i in pieces:
            nc.vector.tensor_tensor(fis[i][:], products[1, i][:], biased[i][:], ADD)

        for group in range(PIECES // STORED):
            keys = staged.tile([P, STORED * PIECE], F32, name="keys")
            values = staged.tile([P, STORED * PIECE], F32, name="values")
            for s in range(STORED):
                fi = fis[group * STORED + s]
                part = slice(s * PIECE, (s + 1) * PIECE)
                keys_bank = banks.tile([P, PIECE], F32, name="keys_bank", tag="bank")
                values_bank = banks.tile([P, PIECE], F32, name="values_bank", tag="bank")
                nc.tensor.matmul(keys_bank[:], to_keys[:], fi[:], start=True, stop=True)
                nc.tensor.matmul(values_bank[:], to_values[:], fi[:], start=True, stop=True)
                nc.scalar.activation(keys[:, part], keys_bank[:], IDENTITY, bias=key_bias[:])
                nc.vector.tensor_scalar(values[:, part], values_bank[:], value_bias[:], None, ADD)
            positions = slice(group * STORED * PIECE, (group + 1) * STORED * PIECE)
            keys_queue = nc.scalar if group == PIECES // STORED - 1 else nc.sync
            keys_queue.dma_start(out[0:P, positions], keys[:])
            nc.sync.dma_start(out[P : 2 * P, positions], values[:])
